import numpy as np
import ml_dtypes


def mxq(x, axis, fmt="e4m3"):
    dtype, down = {"e4m3": (ml_dtypes.float8_e4m3fn, 7), "e5m2": (ml_dtypes.float8_e5m2, 14)}[fmt]
    v = np.moveaxis(np.asarray(x, np.float32).astype(ml_dtypes.bfloat16).astype(np.float64), axis, -1)
    blocks = v.reshape(v.shape[:-1] + (-1, 32))
    amax = np.abs(blocks).max(-1, keepdims=True)
    byte = np.maximum(np.where(amax > 0, np.frexp(amax)[1] - 1 + 127, 0) - down, 1)
    scale = np.exp2(byte - 127.0)
    codes = (blocks / scale).astype(np.float32).astype(dtype).astype(np.float64)
    return np.moveaxis((codes * scale).reshape(v.shape), -1, axis)


WIDE = False


def mx_kscale(k):
    if not WIDE:
        return np.ones(k)
    levels = np.array([10, -10, 5, -5, 0])
    if k % 512:
        return np.exp2(np.random.permutation(np.resize(levels, k // 32))).repeat(32)
    a = np.empty((k // 512, 16))
    for p in range(k // 512):
        a[p, :8] = np.random.permutation(np.resize(levels, 8))
        for g in range(8):
            far = levels[np.abs(levels - a[p, g]) >= 10]
            a[p, g + 8] = far[np.random.randint(len(far))]
    return np.exp2(a.ravel()).repeat(32)


BF16 = ml_dtypes.bfloat16


def bf(x):
    return np.asarray(x, np.float32).astype(BF16)


def f64(x):
    return np.asarray(x).astype(np.float64)


N, D, H, E = 1024, 512, 2048, 8

CLAMP_MAX = float(np.log(100.0))


def setup_inputs():
    s, t = mx_kscale(D), mx_kscale(H)
    return {"x": bf(np.random.standard_normal((N, D)) * s),
            "W1": bf(np.random.standard_normal((E, D, H)) / np.sqrt(D) / s[:, None] * t),
            "b1": bf(np.random.standard_normal((E, H)) * 0.1 * t),
            "W2": bf(np.random.standard_normal((E, H, D)) / np.sqrt(H) / t[:, None]),
            "b2": bf(np.random.standard_normal((E, D)) * 0.1),
            "temperature": bf(np.log(2.0) + 0.1 * np.random.standard_normal((1,)))}


def reference(x, W1, b1, W2, b2, temperature):
    xe = f64(x).reshape(E, N // E, D)
    h = np.maximum((mxq(xe, 2, "e4m3") @ mxq(f64(W1), 1, "e4m3")) + f64(b1)[:, None, :], 0.0)
    y = (mxq(h, 2, "e4m3") @ mxq(f64(W2), 1, "e4m3")) + f64(b2)[:, None, :]
    logit_scale = np.exp(np.minimum(f64(temperature), CLAMP_MAX))
    return y.reshape(N, D) * logit_scale

@@ -1,0 +1,322 @@
+import math
+from contextlib import ExitStack
+
+import concourse.mybir as mybir
+from concourse.masks import make_identity
+
+F32 = mybir.dt.float32
+BF16 = mybir.dt.bfloat16
+U32 = mybir.dt.uint32
+U8 = mybir.dt.uint8
+FP8X4 = mybir.dt.float8_e4m3fn_x4
+ADD = mybir.AluOpType.add
+MULT = mybir.AluOpType.mult
+EXP = mybir.ActivationFunctionType.Exp
+
+E, TOK, D, H = 8, 128, 512, 2048
+P = 128
+FLOPS = 2 * 2 * E * TOK * D * H
+CLAMP_MAX = math.log(100.0)
+
+FAST = False
+V_NUM, V_DEN = 7, 16
+V_COLS = 232
+V_HEAD, N_HEAD = 320, 6
+V_TAIL, N_TAIL = 96, 2
+LOOK = 2
+GRP_BUFS = 6
+CODE_BUFS = 6
+C_OFF = 2
+D_OFF = 4
+RAW_BUFS = 7
+
+
+def v_cols(j):
+    if j < N_HEAD:
+        return V_HEAD
+    if j >= 64 - N_TAIL:
+        return V_TAIL
+    return V_COLS
+
+
+def tile_moelayer_kernel(tc, x, W1, b1, W2, b2, temperature, out):
+    nc = tc.nc
+
+    groups = [("w1", 0)]
+    for e in range(1, E):
+        groups.append(("w1", e))
+        groups.append(("w2", e - 1))
+    groups.append(("w2", E - 1))
+    chunks = [(kind, e, i) for (kind, e) in groups for i in range(4)]
+    n_chunks = len(chunks)
+    first = {}
+    for j, (kind, e, i) in enumerate(chunks):
+        if i == 0:
+            first[(kind, e)] = j
+
+    units = [[0], [1]] + [[j, j + 1] for j in range(2, n_chunks, 2)]
+
+    with ExitStack() as ctx:
+        consts = ctx.enter_context(tc.tile_pool(name="consts", bufs=1))
+        rawp = ctx.enter_context(tc.tile_pool(name="rawp", bufs=RAW_BUFS))
+        grpp = ctx.enter_context(tc.tile_pool(name="grpp", bufs=GRP_BUFS))
+        codep = ctx.enter_context(tc.tile_pool(name="codep", bufs=CODE_BUFS))
+        xp = ctx.enter_context(tc.tile_pool(name="xp", bufs=4))
+        hp = ctx.enter_context(tc.tile_pool(name="hp", bufs=3))
+        yp = ctx.enter_context(tc.tile_pool(name="yp", bufs=3))
+        psum = ctx.enter_context(tc.psum_pool(name="psum", bufs=8))
+        ctx.enter_context(tc.manual_schedule())
+
+        raw_view = {}
+        grp = {}
+        codes = {}
+        scales = {}
+        xraw = {}
+        xgrp = {}
+        xcodes = {}
+        xscales = {}
+        bank = {}
+        hT = {}
+        hsum = {}
+        hrelu = {}
+        hcodes = {}
+        hscales = {}
+        ybank = {}
+        state = {"unit": 0, "done": 0}
+
+        def load_unit(u):
+            js = units[u]
+            kind, e, i0 = chunks[js[0]]
+            n = len(js)
+            raw = rawp.tile([P, n * 2048], BF16, tag="raw", name="raw")
+            if kind == "w1":
+                view = raw[:].rearrange("p (j c) -> p j c", j=4)
+                src = W1[e].rearrange("(p j) c -> p j c", j=4)[:, :, i0 * 512:(i0 + n) * 512]
+                nc.sync.dma_start(out=view, in_=src)
+                for k, j in enumerate(js):
+                    raw_view[j] = view[:, :, k * 512:(k + 1) * 512]
+            else:
+                view = raw[:].rearrange("p (g j c) -> p g j c", g=n, j=4)
+                src = W2[e].rearrange("(g p j) c -> p g j c", p=P, j=4)[:, i0:i0 + n]
+                nc.sync.dma_start(out=view, in_=src)
+                for k, j in enumerate(js):
+                    raw_view[j] = view[:, k]
+
+        def load_x(q):
+            t = xp.tile([P, 1024], BF16, tag="xraw", name="xraw")
+            nc.sync.dma_start(
+                out=t[:].rearrange("p (i k) -> p i k", i=2),
+                in_=x[q * 256:(q + 1) * 256, :].rearrange("(i p) k -> p i k", p=P),
+            )
+            xraw[q] = t
+
+        def loads_allowed():
+            while state["unit"] < len(units):
+                u = state["unit"]
+                if u >= RAW_BUFS and units[u - RAW_BUFS][-1] >= state["done"]:
+                    break
+                load_unit(u)
+                state["unit"] = u + 1
+                if u == 4:
+                    load_x(1)
+                if u == 5:
+                    nc.sync.dma_start(out=b2bc[:], in_=b2.rearrange("e d -> (e d)").partition_broadcast(P))
+
+        def interleave(j):
+            g = grpp.tile([P, 2048], BF16, tag="grp", name="grp", align_bytes=64)
+            src = raw_view[j]
+            if FAST:
+                o = g[:].rearrange("p (c i j) -> p c j i", i=4, j=4)
+                s = src.rearrange("p j (c i) -> p c j i", i=4)
+            else:
+                o = g[:].rearrange("p (c j) -> p c j", j=4)
+                s = src.rearrange("p j c -> p c j")
+            v = v_cols(j) // (4 if FAST else 1)
+            nc.vector.tensor_copy(out=o[:, 0:v], in_=s[:, 0:v])
+            nc.scalar.copy(out=o[:, v:], in_=s[:, v:])
+            grp[j] = g
+            state["done"] = j + 1
+
+        def quantise(j):
+            c = codep.tile([P, 512], U32, tag="codes", name="codes", align_bytes=64)
+            s = codep.tile([P, 512], U8, tag="scales", name="scales", align_bytes=64)
+            nc.vector.quantize_mx(out=c[:].bitcast(FP8X4), scales=s[:], in_=grp[j][:])
+            codes[j] = c
+            scales[j] = s
+
+        def x_turn(q):
+            xt = psum.tile([P, 512], F32, tag="bank", name="xt")
+            words = xraw[q][:].bitcast(F32)
+            for i in range(2):
+                for u in range(2):
+                    k = 2 * i + u
+                    nc.tensor.transpose(xt[:, k * P:(k + 1) * P], words[:, i * 256 + u:(i + 1) * 256:2], ident[:])
+            g = xp.tile([P, 1024], BF16, tag="xgrp", name="xgrp", align_bytes=64)
+            nc.scalar.copy(
+                out=g[:].bitcast(F32).rearrange("p (i r u) -> p i r u", i=2, u=2),
+                in_=xt[:].rearrange("p (i u r) -> p i r u", i=2, u=2),
+            )
+            xgrp[q] = g
+
+        def x_quantise(q):
+            c = xp.tile([P, 256], U32, tag="xcodes", name="xcodes", align_bytes=64)
+            s = xp.tile([P, 256], U8, tag="xscales", name="xscales", align_bytes=64)
+            nc.vector.quantize_mx(out=c[:].bitcast(FP8X4), scales=s[:], in_=xgrp[q][:])
+            xcodes[q] = c
+            xscales[q] = s
+
+        def stage1(j):
+            kind, e, n = chunks[j]
+            b = psum.tile([P, 512], F32, tag="bank", name="bank")
+            cols = slice((e % 2) * P, (e % 2 + 1) * P)
+            nc.tensor.matmul_mx(
+                out=b[:],
+                lhsT=xcodes[e // 2][:, cols].bitcast(FP8X4),
+                lhsT_scale=xscales[e // 2][:, cols],
+                rhs=codes[j][:].bitcast(FP8X4),
+                rhs_scale=scales[j][:],
+                start=True,
+                stop=True,
+            )
+            bank[j] = b
+
+        def h_turn(j):
+            hs = hp.tile([P, 512], F32, tag="hs", name="hs")
+            nc.scalar.copy(
+                out=hs[:].rearrange("p (t m) -> p t m", t=4),
+                in_=bank[j][:].rearrange("p (m t) -> p t m", t=4),
+            )
+            ht = psum.tile([P, 512], F32, tag="bank", name="ht")
+            for t in range(4):
+                nc.tensor.transpose(ht[:, t * P:(t + 1) * P], hs[:, t * P:(t + 1) * P], ident[:])
+            hT[j] = ht
+
+        def h_bias(j):
+            kind, e, n = chunks[j]
+            if n == 0:
+                hsum[e] = hp.tile([P, 2048], BF16, tag="hsum", name="hsum", bufs=2)
+            q = 4 * e + n
+            nc.vector.tensor_tensor(
+                out=hsum[e][:, n * 512:(n + 1) * 512].rearrange("p (r t) -> p r t", t=4),
+                in0=hT[j][:].rearrange("p (t r) -> p r t", t=4),
+                in1=b1_sb[:, 4 * q:4 * q + 4].unsqueeze(1).to_broadcast([P, P, 4]),
+                op=ADD,
+            )
+
+        def h_relu(e):
+            r = hp.tile([P, 2048], BF16, tag="hrelu", name="hrelu", bufs=2, align_bytes=64)
+            nc.vector.tensor_scalar_max(out=r[:], in0=hsum[e][:], scalar1=0.0)
+            hrelu[e] = r
+
+        def h_quantise(e):
+            c = hp.tile([P, 512], U32, tag="hcodes", name="hcodes", align_bytes=64)
+            s = hp.tile([P, 512], U8, tag="hscales", name="hscales", align_bytes=64)
+            nc.vector.quantize_mx(out=c[:].bitcast(FP8X4), scales=s[:], in_=hrelu[e][:])
+            hcodes[e] = c
+            hscales[e] = s
+
+        def stage2(j):
+            kind, e, g = chunks[j]
+            if g == 0:
+                ybank[e] = psum.tile([P, 512], F32, tag="bank", name="ybank")
+            cols = slice(g * P, (g + 1) * P)
+            nc.tensor.matmul_mx(
+                out=ybank[e][:],
+                lhsT=hcodes[e][:, cols].bitcast(FP8X4),
+                lhsT_scale=hscales[e][:, cols],
+                rhs=codes[j][:].bitcast(FP8X4),
+                rhs_scale=scales[j][:],
+                start=(g == 0),
+                stop=(g == 3),
+            )
+
+        def y_out(e):
+            yo = yp.tile([P, 512], F32, tag="yo", name="yo")
+            nc.vector.scalar_tensor_tensor(
+                out=yo[:], in0=ybank[e][:], scalar=s_col[:, 0:1], in1=b2s[:, e * 512:(e + 1) * 512],
+                op0=MULT, op1=ADD,
+            )
+            nc.sync.dma_start(out=out[e * P:(e + 1) * P, :], in_=yo[:])
+
+        warm = consts.tile([P, 1], F32, name="warm")
+        warm2 = consts.tile([P, 1], F32, name="warm2")
+        t_bf = consts.tile([P, 1], BF16, name="t_bf")
+        t_min = consts.tile([P, 1], F32, name="t_min")
+        s_col = consts.tile([P, 1], F32, name="s_col")
+        ident = consts.tile([P, P], F32, name="ident")
+        b1pad = consts.tile([P, 512], BF16, name="b1pad")
+        b1_sb = consts.tile([P, 128], BF16, name="b1_sb")
+        b2bc = consts.tile([P, E * D], BF16, name="b2bc")
+        b2s = consts.tile([P, E * D], F32, name="b2s")
+
+        nc.vector.memset(warm[:], 0.0)
+        nc.scalar.activation(out=warm2[:], in_=warm[:], func=EXP)
+        nc.gpsimd.memset(b1pad[32:64, :], 0.0)
+        nc.gpsimd.memset(b1pad[64:128, :], 0.0)
+        make_identity(nc, ident[:])
+        nc.sync.dma_start(out=t_bf[:], in_=temperature.partition_broadcast(P))
+        nc.sync.dma_start(out=b1pad[0:32, :], in_=b1.rearrange("e (g h) -> (e g) h", g=4))
+        load_unit(0)
+        state["unit"] = 1
+        load_x(0)
+        loads_allowed()
+
+        nc.vector.tensor_scalar_min(out=t_min[:], in0=t_bf[:], scalar1=CLAMP_MAX)
+        nc.scalar.activation(out=s_col[:], in_=t_min[:], func=EXP)
+
+        bt = psum.tile([P, 512], F32, tag="bank", name="bt")
+        b1w = b1pad[:].bitcast(F32)
+        for u in range(2):
+            nc.tensor.transpose(bt[:, u * P:(u + 1) * P], b1w[:, u:256:2], ident[:])
+
+        for i in range(LOOK):
+            interleave(i)
+            loads_allowed()
+            if i == 0:
+                nc.vector.tensor_copy(
+                    out=b1_sb[:].bitcast(F32).rearrange("p (q u) -> p q u", u=2),
+                    in_=bt[:, 0:256].rearrange("p (u q) -> p q u", u=2)[:, 0:32, :],
+                )
+                x_turn(0)
+        x_quantise(0)
+
+        pending = []
+        y_due = {}
+        for j in range(n_chunks + 3):
+            i = j + LOOK
+            if j < n_chunks:
+                quantise(j)
+            if i < n_chunks:
+                interleave(i)
+                loads_allowed()
+            if j == 6:
+                nc.vector.tensor_scalar_mul(out=b2s[:], in0=b2bc[:], scalar1=s_col[:, 0:1])
+            for e in range(E):
+                if j == first[("w1", e)] + D_OFF + 4:
+                    h_relu(e)
+                if j == first[("w1", e)] + D_OFF + 5:
+                    h_quantise(e)
+            if 0 <= j - D_OFF < n_chunks and chunks[j - D_OFF][0] == "w1":
+                h_bias(j - D_OFF)
+            if j in y_due:
+                y_out(y_due[j])
+            if j < n_chunks:
+                if chunks[j][0] == "w1":
+                    stage1(j)
+                else:
+                    pending.append(j)
+            for jj in list(pending):
+                if chunks[jj][1] in hcodes:
+                    stage2(jj)
+                    pending.remove(jj)
+                    if chunks[jj][2] == 3:
+                        y_due[j + 1] = chunks[jj][1]
+            if 0 <= j - C_OFF < n_chunks and chunks[j - C_OFF][0] == "w1":
+                h_turn(j - C_OFF)
+            for q in range(1, 4):
+                if j == 16 * q - 24:
+                    load_x(q)
+                if j == 16 * q - 12:
+                    x_turn(q)
+                if j == 16 * q - 11:
+                    x_quantise(q)

@@ -18,7 +18,7 @@ P = 128
 FLOPS = 2 * 2 * E * TOK * D * H
 CLAMP_MAX = math.log(100.0)
 
-FAST = False
+FAST = True
 V_NUM, V_DEN = 7, 16
 V_COLS = 232
 V_HEAD, N_HEAD = 320, 6

@@ -18,25 +18,17 @@ P = 128
 FLOPS = 2 * 2 * E * TOK * D * H
 CLAMP_MAX = math.log(100.0)
 
-FAST = True
-V_NUM, V_DEN = 7, 16
-V_COLS = 232
-V_HEAD, N_HEAD = 320, 6
-V_TAIL, N_TAIL = 96, 2
-LOOK = 2
-GRP_BUFS = 6
-CODE_BUFS = 6
-C_OFF = 2
-D_OFF = 4
+V_SHARE = 58
+V_HEAD, N_HEAD = 80, 4
+V_TAIL, N_TAIL = 32, 3
+LOOK = 1
+GRP_BUFS = 4
+CODE_BUFS = 4
+C_OFF = 1
+D_OFF = 2
 RAW_BUFS = 7
-
-
-def v_cols(j):
-    if j < N_HEAD:
-        return V_HEAD
-    if j >= 64 - N_TAIL:
-        return V_TAIL
-    return V_COLS
+N_SINGLE_HEAD = 2
+N_SINGLE_TAIL = 2
 
 
 def tile_moelayer_kernel(tc, x, W1, b1, W2, b2, temperature, out):
@@ -49,12 +41,22 @@ def tile_moelayer_kernel(tc, x, W1, b1, W2, b2, temperature, out):
     groups.append(("w2", E - 1))
     chunks = [(kind, e, i) for (kind, e) in groups for i in range(4)]
     n_chunks = len(chunks)
-    first = {}
-    for j, (kind, e, i) in enumerate(chunks):
-        if i == 0:
-            first[(kind, e)] = j
 
-    units = [[0], [1]] + [[j, j + 1] for j in range(2, n_chunks, 2)]
+    units = [[j] for j in range(N_SINGLE_HEAD)]
+    units += [[j, j + 1] for j in range(N_SINGLE_HEAD, n_chunks - N_SINGLE_TAIL, 2)]
+    units += [[j] for j in range(n_chunks - N_SINGLE_TAIL, n_chunks)]
+    n_units = len(units)
+    unit_of = {}
+    for u, js in enumerate(units):
+        for k, j in enumerate(js):
+            unit_of[j] = (u, k)
+
+    def share(u):
+        if u < N_HEAD:
+            return V_HEAD
+        if u >= n_units - N_TAIL:
+            return V_TAIL
+        return V_SHARE
 
     with ExitStack() as ctx:
         consts = ctx.enter_context(tc.tile_pool(name="consts", bufs=1))
@@ -62,12 +64,12 @@ def tile_moelayer_kernel(tc, x, W1, b1, W2, b2, temperature, out):
         grpp = ctx.enter_context(tc.tile_pool(name="grpp", bufs=GRP_BUFS))
         codep = ctx.enter_context(tc.tile_pool(name="codep", bufs=CODE_BUFS))
         xp = ctx.enter_context(tc.tile_pool(name="xp", bufs=4))
-        hp = ctx.enter_context(tc.tile_pool(name="hp", bufs=3))
+        hp = ctx.enter_context(tc.tile_pool(name="hp", bufs=4))
         yp = ctx.enter_context(tc.tile_pool(name="yp", bufs=3))
         psum = ctx.enter_context(tc.psum_pool(name="psum", bufs=8))
         ctx.enter_context(tc.manual_schedule())
 
-        raw_view = {}
+        raw = {}
         grp = {}
         codes = {}
         scales = {}
@@ -88,19 +90,18 @@ def tile_moelayer_kernel(tc, x, W1, b1, W2, b2, temperature, out):
             js = units[u]
             kind, e, i0 = chunks[js[0]]
             n = len(js)
-            raw = rawp.tile([P, n * 2048], BF16, tag="raw", name="raw")
+            t = rawp.tile([P, n * 2048], BF16, tag="raw", name="raw")
             if kind == "w1":
-                view = raw[:].rearrange("p (j c) -> p j c", j=4)
-                src = W1[e].rearrange("(p j) c -> p j c", j=4)[:, :, i0 * 512:(i0 + n) * 512]
-                nc.sync.dma_start(out=view, in_=src)
-                for k, j in enumerate(js):
-                    raw_view[j] = view[:, :, k * 512:(k + 1) * 512]
+                nc.sync.dma_start(
+                    out=t[:].rearrange("p (j c) -> p j c", j=4),
+                    in_=W1[e].rearrange("(p j) c -> p j c", j=4)[:, :, i0 * 512:(i0 + n) * 512],
+                )
             else:
-                view = raw[:].rearrange("p (g j c) -> p g j c", g=n, j=4)
-                src = W2[e].rearrange("(g p j) c -> p g j c", p=P, j=4)[:, i0:i0 + n]
-                nc.sync.dma_start(out=view, in_=src)
-                for k, j in enumerate(js):
-                    raw_view[j] = view[:, k]
+                nc.sync.dma_start(
+                    out=t[:].rearrange("p (g j c) -> p g j c", g=n, j=4),
+                    in_=W2[e].rearrange("(g p j) c -> p g j c", p=P, j=4)[:, i0:i0 + n],
+                )
+            raw[u] = t
 
         def load_x(q):
             t = xp.tile([P, 1024], BF16, tag="xraw", name="xraw")
@@ -111,9 +112,9 @@ def tile_moelayer_kernel(tc, x, W1, b1, W2, b2, temperature, out):
             xraw[q] = t
 
         def loads_allowed():
-            while state["unit"] < len(units):
+            while state["unit"] < n_units:
                 u = state["unit"]
-                if u >= RAW_BUFS and units[u - RAW_BUFS][-1] >= state["done"]:
+                if u >= RAW_BUFS and u - RAW_BUFS >= state["done"]:
                     break
                 load_unit(u)
                 state["unit"] = u + 1
@@ -122,35 +123,42 @@ def tile_moelayer_kernel(tc, x, W1, b1, W2, b2, temperature, out):
                 if u == 5:
                     nc.sync.dma_start(out=b2bc[:], in_=b2.rearrange("e d -> (e d)").partition_broadcast(P))
 
-        def interleave(j):
-            g = grpp.tile([P, 2048], BF16, tag="grp", name="grp", align_bytes=64)
-            src = raw_view[j]
-            if FAST:
+        def interleave(u):
+            js = units[u]
+            n = len(js)
+            kind = chunks[js[0]][0]
+            g = grpp.tile([P, n * 2048], BF16, tag="grp", name="grp", align_bytes=64)
+            v = share(u) * n
+            if kind == "w1":
                 o = g[:].rearrange("p (c i j) -> p c j i", i=4, j=4)
-                s = src.rearrange("p j (c i) -> p c j i", i=4)
+                s = raw[u][:].rearrange("p (j c i) -> p c j i", j=4, i=4)
+                nc.vector.tensor_copy(out=o[:, 0:v], in_=s[:, 0:v])
+                nc.scalar.copy(out=o[:, v:], in_=s[:, v:])
             else:
-                o = g[:].rearrange("p (c j) -> p c j", j=4)
-                s = src.rearrange("p j c -> p c j")
-            v = v_cols(j) // (4 if FAST else 1)
-            nc.vector.tensor_copy(out=o[:, 0:v], in_=s[:, 0:v])
-            nc.scalar.copy(out=o[:, v:], in_=s[:, v:])
-            grp[j] = g
-            state["done"] = j + 1
+                o = g[:].rearrange("p (g c i j) -> p g c j i", g=n, i=4, j=4)
+                s = raw[u][:].rearrange("p (g j c i) -> p g c j i", g=n, j=4, i=4)
+                nc.vector.tensor_copy(out=o[:, 0, 0:v], in_=s[:, 0, 0:v])
+                nc.scalar.copy(out=o[:, 0, v:], in_=s[:, 0, v:])
+                if n == 2:
+                    nc.scalar.copy(out=o[:, 1], in_=s[:, 1])
+            grp[u] = g
+            state["done"] = u + 1
 
-        def quantise(j):
-            c = codep.tile([P, 512], U32, tag="codes", name="codes", align_bytes=64)
-            s = codep.tile([P, 512], U8, tag="scales", name="scales", align_bytes=64)
-            nc.vector.quantize_mx(out=c[:].bitcast(FP8X4), scales=s[:], in_=grp[j][:])
-            codes[j] = c
-            scales[j] = s
+        def quantise(u):
+            n = len(units[u])
+            c = codep.tile([P, n * 512], U32, tag="codes", name="codes", align_bytes=64)
+            s = codep.tile([P, n * 512], U8, tag="scales", name="scales", align_bytes=64)
+            nc.vector.quantize_mx(out=c[:].bitcast(FP8X4), scales=s[:], in_=grp[u][:])
+            codes[u] = c
+            scales[u] = s
 
         def x_turn(q):
             xt = psum.tile([P, 512], F32, tag="bank", name="xt")
             words = xraw[q][:].bitcast(F32)
             for i in range(2):
-                for u in range(2):
-                    k = 2 * i + u
-                    nc.tensor.transpose(xt[:, k * P:(k + 1) * P], words[:, i * 256 + u:(i + 1) * 256:2], ident[:])
+                for w in range(2):
+                    k = 2 * i + w
+                    nc.tensor.transpose(xt[:, k * P:(k + 1) * P], words[:, i * 256 + w:(i + 1) * 256:2], ident[:])
             g = xp.tile([P, 1024], BF16, tag="xgrp", name="xgrp", align_bytes=64)
             nc.scalar.copy(
                 out=g[:].bitcast(F32).rearrange("p (i r u) -> p i r u", i=2, u=2),
@@ -167,14 +175,16 @@ def tile_moelayer_kernel(tc, x, W1, b1, W2, b2, temperature, out):
 
         def stage1(j):
             kind, e, n = chunks[j]
+            u, k = unit_of[j]
             b = psum.tile([P, 512], F32, tag="bank", name="bank")
             cols = slice((e % 2) * P, (e % 2 + 1) * P)
+            wcols = slice(k * 512, (k + 1) * 512)
             nc.tensor.matmul_mx(
                 out=b[:],
                 lhsT=xcodes[e // 2][:, cols].bitcast(FP8X4),
                 lhsT_scale=xscales[e // 2][:, cols],
-                rhs=codes[j][:].bitcast(FP8X4),
-                rhs_scale=scales[j][:],
+                rhs=codes[u][:, wcols].bitcast(FP8X4),
+                rhs_scale=scales[u][:, wcols],
                 start=True,
                 stop=True,
             )
@@ -209,23 +219,25 @@ def tile_moelayer_kernel(tc, x, W1, b1, W2, b2, temperature, out):
             hrelu[e] = r
 
         def h_quantise(e):
-            c = hp.tile([P, 512], U32, tag="hcodes", name="hcodes", align_bytes=64)
-            s = hp.tile([P, 512], U8, tag="hscales", name="hscales", align_bytes=64)
+            c = hp.tile([P, 512], U32, tag="hcodes", name="hcodes", bufs=3, align_bytes=64)
+            s = hp.tile([P, 512], U8, tag="hscales", name="hscales", bufs=3, align_bytes=64)
             nc.vector.quantize_mx(out=c[:].bitcast(FP8X4), scales=s[:], in_=hrelu[e][:])
             hcodes[e] = c
             hscales[e] = s
 
         def stage2(j):
             kind, e, g = chunks[j]
+            u, k = unit_of[j]
             if g == 0:
                 ybank[e] = psum.tile([P, 512], F32, tag="bank", name="ybank")
             cols = slice(g * P, (g + 1) * P)
+            wcols = slice(k * 512, (k + 1) * 512)
             nc.tensor.matmul_mx(
                 out=ybank[e][:],
                 lhsT=hcodes[e][:, cols].bitcast(FP8X4),
                 lhsT_scale=hscales[e][:, cols],
-                rhs=codes[j][:].bitcast(FP8X4),
-                rhs_scale=scales[j][:],
+                rhs=codes[u][:, wcols].bitcast(FP8X4),
+                rhs_scale=scales[u][:, wcols],
                 start=(g == 0),
                 stop=(g == 3),
             )
@@ -266,57 +278,62 @@ def tile_moelayer_kernel(tc, x, W1, b1, W2, b2, temperature, out):
 
         bt = psum.tile([P, 512], F32, tag="bank", name="bt")
         b1w = b1pad[:].bitcast(F32)
-        for u in range(2):
-            nc.tensor.transpose(bt[:, u * P:(u + 1) * P], b1w[:, u:256:2], ident[:])
+        for w in range(2):
+            nc.tensor.transpose(bt[:, w * P:(w + 1) * P], b1w[:, w:256:2], ident[:])
+        nc.vector.tensor_copy(
+            out=b1_sb[:].bitcast(F32).rearrange("p (q u) -> p q u", u=2),
+            in_=bt[:, 0:256].rearrange("p (u q) -> p q u", u=2)[:, 0:32, :],
+        )
+
+        def b2_scale(arg):
+            nc.vector.tensor_scalar_mul(out=b2s[:], in0=b2bc[:], scalar1=s_col[:, 0:1])
 
         for i in range(LOOK):
             interleave(i)
             loads_allowed()
             if i == 0:
-                nc.vector.tensor_copy(
-                    out=b1_sb[:].bitcast(F32).rearrange("p (q u) -> p q u", u=2),
-                    in_=bt[:, 0:256].rearrange("p (u q) -> p q u", u=2)[:, 0:32, :],
-                )
                 x_turn(0)
         x_quantise(0)
 
         pending = []
-        y_due = {}
-        for j in range(n_chunks + 3):
-            i = j + LOOK
-            if j < n_chunks:
-                quantise(j)
-            if i < n_chunks:
+        events = {}
+
+        def at(slot, fn, arg):
+            events.setdefault(slot, []).append((fn, arg))
+
+        at(6, b2_scale, 0)
+        for q in range(1, 4):
+            j0 = 16 * q - 4
+            u0 = unit_of[j0][0]
+            if q > 1:
+                at(u0 - 10, load_x, q)
+            at(u0 - 4, x_turn, q)
+            at(u0 - 3, x_quantise, q)
+
+        for u in range(n_units + 4):
+            i = u + LOOK
+            if u < n_units:
+                quantise(u)
+            if i < n_units:
                 interleave(i)
                 loads_allowed()
-            if j == 6:
-                nc.vector.tensor_scalar_mul(out=b2s[:], in0=b2bc[:], scalar1=s_col[:, 0:1])
-            for e in range(E):
-                if j == first[("w1", e)] + D_OFF + 4:
-                    h_relu(e)
-                if j == first[("w1", e)] + D_OFF + 5:
-                    h_quantise(e)
-            if 0 <= j - D_OFF < n_chunks and chunks[j - D_OFF][0] == "w1":
-                h_bias(j - D_OFF)
-            if j in y_due:
-                y_out(y_due[j])
-            if j < n_chunks:
-                if chunks[j][0] == "w1":
-                    stage1(j)
-                else:
-                    pending.append(j)
+            for (fn, arg) in events.get(u, []):
+                fn(arg)
+            if u < n_units:
+                for j in units[u]:
+                    kind, e, n = chunks[j]
+                    if kind == "w1":
+                        stage1(j)
+                        at(u + C_OFF, h_turn, j)
+                        at(u + D_OFF, h_bias, j)
+                        if n == 3:
+                            at(u + D_OFF + 1, h_relu, e)
+                            at(u + D_OFF + 2, h_quantise, e)
+                    else:
+                        pending.append(j)
             for jj in list(pending):
                 if chunks[jj][1] in hcodes:
                     stage2(jj)
                     pending.remove(jj)
                     if chunks[jj][2] == 3:
-                        y_due[j + 1] = chunks[jj][1]
-            if 0 <= j - C_OFF < n_chunks and chunks[j - C_OFF][0] == "w1":
-                h_turn(j - C_OFF)
-            for q in range(1, 4):
-                if j == 16 * q - 24:
-                    load_x(q)
-                if j == 16 * q - 12:
-                    x_turn(q)
-                if j == 16 * q - 11:
-                    x_quantise(q)
+                        at(u + 1, y_out, chunks[jj][1])

import math
from contextlib import ExitStack

import concourse.mybir as mybir
from concourse.masks import make_identity

F32 = mybir.dt.float32
BF16 = mybir.dt.bfloat16
U32 = mybir.dt.uint32
U8 = mybir.dt.uint8
FP8X4 = mybir.dt.float8_e4m3fn_x4
ADD = mybir.AluOpType.add
MULT = mybir.AluOpType.mult
EXP = mybir.ActivationFunctionType.Exp

E, TOK, D, H = 8, 128, 512, 2048
P = 128
FLOPS = 2 * 2 * E * TOK * D * H
CLAMP_MAX = math.log(100.0)

V_SHARE = 58
V_HEAD, N_HEAD = 80, 4
V_TAIL, N_TAIL = 32, 3
LOOK = 1
GRP_BUFS = 4
CODE_BUFS = 4
C_OFF = 1
D_OFF = 2
RAW_BUFS = 7
N_SINGLE_HEAD = 2
N_SINGLE_TAIL = 2


def tile_moelayer_kernel(tc, x, W1, b1, W2, b2, temperature, out):
    nc = tc.nc

    groups = [("w1", 0)]
    for e in range(1, E):
        groups.append(("w1", e))
        groups.append(("w2", e - 1))
    groups.append(("w2", E - 1))
    chunks = [(kind, e, i) for (kind, e) in groups for i in range(4)]
    n_chunks = len(chunks)

    units = [[j] for j in range(N_SINGLE_HEAD)]
    units += [[j, j + 1] for j in range(N_SINGLE_HEAD, n_chunks - N_SINGLE_TAIL, 2)]
    units += [[j] for j in range(n_chunks - N_SINGLE_TAIL, n_chunks)]
    n_units = len(units)
    unit_of = {}
    for u, js in enumerate(units):
        for k, j in enumerate(js):
            unit_of[j] = (u, k)

    def share(u):
        if u < N_HEAD:
            return V_HEAD
        if u >= n_units - N_TAIL:
            return V_TAIL
        return V_SHARE

    with ExitStack() as ctx:
        consts = ctx.enter_context(tc.tile_pool(name="consts", bufs=1))
        rawp = ctx.enter_context(tc.tile_pool(name="rawp", bufs=RAW_BUFS))
        grpp = ctx.enter_context(tc.tile_pool(name="grpp", bufs=GRP_BUFS))
        codep = ctx.enter_context(tc.tile_pool(name="codep", bufs=CODE_BUFS))
        xp = ctx.enter_context(tc.tile_pool(name="xp", bufs=4))
        hp = ctx.enter_context(tc.tile_pool(name="hp", bufs=4))
        yp = ctx.enter_context(tc.tile_pool(name="yp", bufs=3))
        psum = ctx.enter_context(tc.psum_pool(name="psum", bufs=8))
        ctx.enter_context(tc.manual_schedule())

        raw = {}
        grp = {}
        codes = {}
        scales = {}
        xraw = {}
        xgrp = {}
        xcodes = {}
        xscales = {}
        bank = {}
        hT = {}
        hsum = {}
        hrelu = {}
        hcodes = {}
        hscales = {}
        ybank = {}
        state = {"unit": 0, "done": 0}

        def load_unit(u):
            js = units[u]
            kind, e, i0 = chunks[js[0]]
            n = len(js)
            t = rawp.tile([P, n * 2048], BF16, tag="raw", name="raw")
            if kind == "w1":
                nc.sync.dma_start(
                    out=t[:].rearrange("p (j c) -> p j c", j=4),
                    in_=W1[e].rearrange("(p j) c -> p j c", j=4)[:, :, i0 * 512:(i0 + n) * 512],
                )
            else:
                nc.sync.dma_start(
                    out=t[:].rearrange("p (g j c) -> p g j c", g=n, j=4),
                    in_=W2[e].rearrange("(g p j) c -> p g j c", p=P, j=4)[:, i0:i0 + n],
                )
            raw[u] = t

        def load_x(q):
            t = xp.tile([P, 1024], BF16, tag="xraw", name="xraw")
            nc.sync.dma_start(
                out=t[:].rearrange("p (i k) -> p i k", i=2),
                in_=x[q * 256:(q + 1) * 256, :].rearrange("(i p) k -> p i k", p=P),
            )
            xraw[q] = t

        def loads_allowed():
            while state["unit"] < n_units:
                u = state["unit"]
                if u >= RAW_BUFS and u - RAW_BUFS >= state["done"]:
                    break
                load_unit(u)
                state["unit"] = u + 1
                if u == 4:
                    load_x(1)
                if u == 5:
                    nc.sync.dma_start(out=b2bc[:], in_=b2.rearrange("e d -> (e d)").partition_broadcast(P))

        def interleave(u):
            js = units[u]
            n = len(js)
            kind = chunks[js[0]][0]
            g = grpp.tile([P, n * 2048], BF16, tag="grp", name="grp", align_bytes=64)
            v = share(u) * n
            if kind == "w1":
                o = g[:].rearrange("p (c i j) -> p c j i", i=4, j=4)
                s = raw[u][:].rearrange("p (j c i) -> p c j i", j=4, i=4)
                nc.vector.tensor_copy(out=o[:, 0:v], in_=s[:, 0:v])
                nc.scalar.copy(out=o[:, v:], in_=s[:, v:])
            else:
                o = g[:].rearrange("p (g c i j) -> p g c j i", g=n, i=4, j=4)
                s = raw[u][:].rearrange("p (g j c i) -> p g c j i", g=n, j=4, i=4)
                nc.vector.tensor_copy(out=o[:, 0, 0:v], in_=s[:, 0, 0:v])
                nc.scalar.copy(out=o[:, 0, v:], in_=s[:, 0, v:])
                if n == 2:
                    nc.scalar.copy(out=o[:, 1], in_=s[:, 1])
            grp[u] = g
            state["done"] = u + 1

        def quantise(u):
            n = len(units[u])
            c = codep.tile([P, n * 512], U32, tag="codes", name="codes", align_bytes=64)
            s = codep.tile([P, n * 512], U8, tag="scales", name="scales", align_bytes=64)
            nc.vector.quantize_mx(out=c[:].bitcast(FP8X4), scales=s[:], in_=grp[u][:])
            codes[u] = c
            scales[u] = s

        def x_turn(q):
            xt = psum.tile([P, 512], F32, tag="bank", name="xt")
            words = xraw[q][:].bitcast(F32)
            for i in range(2):
                for w in range(2):
                    k = 2 * i + w
                    nc.tensor.transpose(xt[:, k * P:(k + 1) * P], words[:, i * 256 + w:(i + 1) * 256:2], ident[:])
            g = xp.tile([P, 1024], BF16, tag="xgrp", name="xgrp", align_bytes=64)
            nc.scalar.copy(
                out=g[:].bitcast(F32).rearrange("p (i r u) -> p i r u", i=2, u=2),
                in_=xt[:].rearrange("p (i u r) -> p i r u", i=2, u=2),
            )
            xgrp[q] = g

        def x_quantise(q):
            c = xp.tile([P, 256], U32, tag="xcodes", name="xcodes", align_bytes=64)
            s = xp.tile([P, 256], U8, tag="xscales", name="xscales", align_bytes=64)
            nc.vector.quantize_mx(out=c[:].bitcast(FP8X4), scales=s[:], in_=xgrp[q][:])
            xcodes[q] = c
            xscales[q] = s

        def stage1(j):
            kind, e, n = chunks[j]
            u, k = unit_of[j]
            b = psum.tile([P, 512], F32, tag="bank", name="bank")
            cols = slice((e % 2) * P, (e % 2 + 1) * P)
            wcols = slice(k * 512, (k + 1) * 512)
            nc.tensor.matmul_mx(
                out=b[:],
                lhsT=xcodes[e // 2][:, cols].bitcast(FP8X4),
                lhsT_scale=xscales[e // 2][:, cols],
                rhs=codes[u][:, wcols].bitcast(FP8X4),
                rhs_scale=scales[u][:, wcols],
                start=True,
                stop=True,
            )
            bank[j] = b

        def h_turn(j):
            hs = hp.tile([P, 512], F32, tag="hs", name="hs")
            nc.scalar.copy(
                out=hs[:].rearrange("p (t m) -> p t m", t=4),
                in_=bank[j][:].rearrange("p (m t) -> p t m", t=4),
            )
            ht = psum.tile([P, 512], F32, tag="bank", name="ht")
            for t in range(4):
                nc.tensor.transpose(ht[:, t * P:(t + 1) * P], hs[:, t * P:(t + 1) * P], ident[:])
            hT[j] = ht

        def h_bias(j):
            kind, e, n = chunks[j]
            if n == 0:
                hsum[e] = hp.tile([P, 2048], BF16, tag="hsum", name="hsum", bufs=2)
            q = 4 * e + n
            nc.vector.tensor_tensor(
                out=hsum[e][:, n * 512:(n + 1) * 512].rearrange("p (r t) -> p r t", t=4),
                in0=hT[j][:].rearrange("p (t r) -> p r t", t=4),
                in1=b1_sb[:, 4 * q:4 * q + 4].unsqueeze(1).to_broadcast([P, P, 4]),
                op=ADD,
            )

        def h_relu(e):
            r = hp.tile([P, 2048], BF16, tag="hrelu", name="hrelu", bufs=2, align_bytes=64)
            nc.vector.tensor_scalar_max(out=r[:], in0=hsum[e][:], scalar1=0.0)
            hrelu[e] = r

        def h_quantise(e):
            c = hp.tile([P, 512], U32, tag="hcodes", name="hcodes", bufs=3, align_bytes=64)
            s = hp.tile([P, 512], U8, tag="hscales", name="hscales", bufs=3, align_bytes=64)
            nc.vector.quantize_mx(out=c[:].bitcast(FP8X4), scales=s[:], in_=hrelu[e][:])
            hcodes[e] = c
            hscales[e] = s

        def stage2(j):
            kind, e, g = chunks[j]
            u, k = unit_of[j]
            if g == 0:
                ybank[e] = psum.tile([P, 512], F32, tag="bank", name="ybank")
            cols = slice(g * P, (g + 1) * P)
            wcols = slice(k * 512, (k + 1) * 512)
            nc.tensor.matmul_mx(
                out=ybank[e][:],
                lhsT=hcodes[e][:, cols].bitcast(FP8X4),
                lhsT_scale=hscales[e][:, cols],
                rhs=codes[u][:, wcols].bitcast(FP8X4),
                rhs_scale=scales[u][:, wcols],
                start=(g == 0),
                stop=(g == 3),
            )

        def y_out(e):
            yo = yp.tile([P, 512], F32, tag="yo", name="yo")
            nc.vector.scalar_tensor_tensor(
                out=yo[:], in0=ybank[e][:], scalar=s_col[:, 0:1], in1=b2s[:, e * 512:(e + 1) * 512],
                op0=MULT, op1=ADD,
            )
            nc.sync.dma_start(out=out[e * P:(e + 1) * P, :], in_=yo[:])

        warm = consts.tile([P, 1], F32, name="warm")
        warm2 = consts.tile([P, 1], F32, name="warm2")
        t_bf = consts.tile([P, 1], BF16, name="t_bf")
        t_min = consts.tile([P, 1], F32, name="t_min")
        s_col = consts.tile([P, 1], F32, name="s_col")
        ident = consts.tile([P, P], F32, name="ident")
        b1pad = consts.tile([P, 512], BF16, name="b1pad")
        b1_sb = consts.tile([P, 128], BF16, name="b1_sb")
        b2bc = consts.tile([P, E * D], BF16, name="b2bc")
        b2s = consts.tile([P, E * D], F32, name="b2s")

        nc.vector.memset(warm[:], 0.0)
        nc.scalar.activation(out=warm2[:], in_=warm[:], func=EXP)
        nc.gpsimd.memset(b1pad[32:64, :], 0.0)
        nc.gpsimd.memset(b1pad[64:128, :], 0.0)
        make_identity(nc, ident[:])
        nc.sync.dma_start(out=t_bf[:], in_=temperature.partition_broadcast(P))
        nc.sync.dma_start(out=b1pad[0:32, :], in_=b1.rearrange("e (g h) -> (e g) h", g=4))
        load_unit(0)
        state["unit"] = 1
        load_x(0)
        loads_allowed()

        nc.vector.tensor_scalar_min(out=t_min[:], in0=t_bf[:], scalar1=CLAMP_MAX)
        nc.scalar.activation(out=s_col[:], in_=t_min[:], func=EXP)

        bt = psum.tile([P, 512], F32, tag="bank", name="bt")
        b1w = b1pad[:].bitcast(F32)
        for w in range(2):
            nc.tensor.transpose(bt[:, w * P:(w + 1) * P], b1w[:, w:256:2], ident[:])
        nc.vector.tensor_copy(
            out=b1_sb[:].bitcast(F32).rearrange("p (q u) -> p q u", u=2),
            in_=bt[:, 0:256].rearrange("p (u q) -> p q u", u=2)[:, 0:32, :],
        )

        def b2_scale(arg):
            nc.vector.tensor_scalar_mul(out=b2s[:], in0=b2bc[:], scalar1=s_col[:, 0:1])

        for i in range(LOOK):
            interleave(i)
            loads_allowed()
            if i == 0:
                x_turn(0)
        x_quantise(0)

        pending = []
        events = {}

        def at(slot, fn, arg):
            events.setdefault(slot, []).append((fn, arg))

        at(6, b2_scale, 0)
        for q in range(1, 4):
            j0 = 16 * q - 4
            u0 = unit_of[j0][0]
            if q > 1:
                at(u0 - 10, load_x, q)
            at(u0 - 4, x_turn, q)
            at(u0 - 3, x_quantise, q)

        for u in range(n_units + 4):
            i = u + LOOK
            if u < n_units:
                quantise(u)
            if i < n_units:
                interleave(i)
                loads_allowed()
            for (fn, arg) in events.get(u, []):
                fn(arg)
            if u < n_units:
                for j in units[u]:
                    kind, e, n = chunks[j]
                    if kind == "w1":
                        stage1(j)
                        at(u + C_OFF, h_turn, j)
                        at(u + D_OFF, h_bias, j)
                        if n == 3:
                            at(u + D_OFF + 1, h_relu, e)
                            at(u + D_OFF + 2, h_quantise, e)
                    else:
                        pending.append(j)
            for jj in list(pending):
                if chunks[jj][1] in hcodes:
                    stage2(jj)
                    pending.remove(jj)
                    if chunks[jj][2] == 3:
                        at(u + 1, y_out, chunks[jj][1])
